import numpy as np
import ml_dtypes


def mxq(x, axis, fmt="e4m3"):
    dtype, down = {"e4m3": (ml_dtypes.float8_e4m3fn, 7), "e5m2": (ml_dtypes.float8_e5m2, 14)}[fmt]
    v = np.moveaxis(np.asarray(x, np.float32).astype(ml_dtypes.bfloat16).astype(np.float64), axis, -1)
    blocks = v.reshape(v.shape[:-1] + (-1, 32))
    amax = np.abs(blocks).max(-1, keepdims=True)
    byte = np.maximum(np.where(amax > 0, np.frexp(amax)[1] - 1 + 127, 0) - down, 1)
    scale = np.exp2(byte - 127.0)
    codes = (blocks / scale).astype(np.float32).astype(dtype).astype(np.float64)
    return np.moveaxis((codes * scale).reshape(v.shape), -1, axis)


WIDE = False


def mx_kscale(k):
    if not WIDE:
        return np.ones(k)
    levels = np.array([10, -10, 5, -5, 0])
    if k % 512:
        return np.exp2(np.random.permutation(np.resize(levels, k // 32))).repeat(32)
    a = np.empty((k // 512, 16))
    for p in range(k // 512):
        a[p, :8] = np.random.permutation(np.resize(levels, 8))
        for g in range(8):
            far = levels[np.abs(levels - a[p, g]) >= 10]
            a[p, g + 8] = far[np.random.randint(len(far))]
    return np.exp2(a.ravel()).repeat(32)


BF16 = ml_dtypes.bfloat16


def bf(x):
    return np.asarray(x, np.float32).astype(BF16)


def f64(x):
    return np.asarray(x).astype(np.float64)


B, S, D, DFF, R = 4, 160, 256, 16384, 512


def setup_inputs():
    t, r = mx_kscale(DFF), mx_kscale(R)
    v = np.random.standard_normal((B, S, DFF)) * 1.2
    return {"h_gelu": bf(v / (1.0 + np.exp(-1.702 * v)) * t),
            "c_proj_U": bf(np.random.standard_normal((DFF, R)) * 2.0 / np.sqrt(DFF) / t[:, None]),
            "c_proj_S": bf(np.random.uniform(size=R) * r),
            "c_proj_V": bf(np.random.standard_normal((D, R)) / np.sqrt(R) / r[None, :]),
            "c_proj_bias": bf(np.random.standard_normal(D) * 0.3)}


def reference(h_gelu, c_proj_U, c_proj_S, c_proj_V, c_proj_bias):
    us = f64(c_proj_U) * f64(c_proj_S)[None, :]
    w = mxq(us, 1, "e4m3") @ mxq(f64(c_proj_V), 1, "e4m3").T
    return (mxq(f64(h_gelu), 2, "e4m3") @ mxq(w, 0, "e4m3")) + f64(c_proj_bias)

@@ -1,0 +1,288 @@
+from contextlib import ExitStack
+
+import concourse.mybir as mybir
+from concourse.masks import make_identity
+
+BF16 = mybir.dt.bfloat16
+F32 = mybir.dt.float32
+U32 = mybir.dt.uint32
+U8 = mybir.dt.uint8
+FP8X4 = mybir.dt.float8_e4m3fn_x4
+
+P = 128
+PACK = 4
+K_PASS = P * PACK
+
+TOKENS = 640
+TOKEN_BLOCKS = TOKENS // P
+DFF = 16384
+RANK = 512
+D = 256
+D_HALVES = D // P
+PASSES = DFF // K_PASS
+
+BANK_F32 = 512
+BANK_COLS = BANK_F32 // 2
+MOVING_TOKENS = BANK_F32
+MOVING_BLOCKS = MOVING_TOKENS // P
+ACC_BANKS = D_HALVES + 1
+RING_BANKS = 8 - ACC_BANKS
+
+PASSES_PER_LOAD = 2
+LOADS_AHEAD = 6
+LOAD_K = PASSES_PER_LOAD * K_PASS
+
+FLOPS = 2 * DFF * RANK * D + 2 * TOKENS * DFF * D
+
+
+def tile_hybridsuperlayer_pb_k_kernel(
+    tc, h_gelu, c_proj_U, c_proj_S, c_proj_V, c_proj_bias, out
+):
+    nc = tc.nc
+    mult = mybir.AluOpType.mult
+    add = mybir.AluOpType.add
+
+    h_flat = h_gelu.flatten_outer_dims()
+    out_view = out.flatten_outer_dims().rearrange("(b p) d -> p b d", p=P)
+
+    load_first = list(range(PASSES_PER_LOAD)) + list(range(PASSES_PER_LOAD, PASSES, PASSES_PER_LOAD))
+    load_end = load_first[1:] + [PASSES]
+    home = {}
+    for i in range(len(load_first)):
+        for g in range(load_first[i], load_end[i]):
+            home[g] = (i, g - load_first[i])
+
+    with ExitStack() as ctx:
+        consts = ctx.enter_context(tc.tile_pool(name="consts", bufs=1))
+        loads = ctx.enter_context(tc.tile_pool(name="loads", bufs=LOADS_AHEAD))
+        work = ctx.enter_context(tc.tile_pool(name="work", bufs=3))
+        acc_pool = ctx.enter_context(tc.psum_pool(name="acc", bufs=1))
+        ring = ctx.enter_context(tc.psum_pool(name="ring", bufs=RING_BANKS))
+        ctx.enter_context(tc.manual_schedule())
+
+        u_rows = {}
+        h_rows = {}
+
+        def load(i):
+            passes = load_end[i] - load_first[i]
+            k_range = slice(load_first[i] * K_PASS, load_end[i] * K_PASS)
+            h_rows[i] = loads.tile([P, TOKEN_BLOCKS, LOAD_K], BF16, name="h_rows")
+            nc.sync.dma_start(
+                out=h_rows[i][:, :, 0 : passes * K_PASS],
+                in_=h_flat[:, k_range].rearrange("(b p) k -> p b k", p=P),
+            )
+            u_rows[i] = loads.tile([P, PASSES_PER_LOAD, PACK * RANK], BF16, name="u_rows")
+            nc.sync.dma_start(
+                out=u_rows[i][:, 0:passes, :],
+                in_=c_proj_U[k_range, :].rearrange("(x p t) r -> p x (t r)", p=P, t=PACK),
+            )
+
+        v_rows = consts.tile([P, D_HALVES, RANK], BF16)
+        nc.scalar.dma_start(out=v_rows[:], in_=c_proj_V.rearrange("(x p) r -> p x r", p=P))
+        s_word = consts.tile([P, 2, 2], BF16)
+        with nc.allow_non_contiguous_dma(reason="512 values, two pairs to a partition, once"):
+            nc.scalar.dma_start(
+                out=s_word[:], in_=c_proj_S.rearrange("(p half e) -> p half e", half=2, p=P, e=2)
+            )
+        bias_all = consts.tile([P, D], BF16)
+        nc.scalar.dma_start(out=bias_all[:], in_=c_proj_bias.partition_broadcast(P))
+        for i in range(LOADS_AHEAD):
+            load(i)
+
+        ident = consts.tile([P, P], F32)
+        make_identity(nc, ident[:])
+
+        s_bank = consts.tile([P, BANK_COLS, 2, 2], BF16)
+        nc.vector.tensor_copy(
+            out=s_bank[:], in_=s_word[:].unsqueeze(1).to_broadcast([P, BANK_COLS, 2, 2])
+        )
+
+        v_words = v_rows[:].bitcast(F32)
+        v_bank = ring.tile([P, 2, BANK_COLS], F32, tag="bank")
+        for x in range(D_HALVES):
+            for half in range(2):
+                nc.tensor.transpose(
+                    v_bank[:, half, x * P : (x + 1) * P],
+                    v_words[:, x, half : RANK // 2 : 2],
+                    ident[:],
+                )
+        v_t = consts.tile([P, D, PACK], BF16, align_bytes=64)
+        nc.scalar.copy(out=v_t[:].bitcast(F32), in_=v_bank[:].rearrange("p half c -> p c half"))
+        v_codes = consts.tile([P, D], U32, align_bytes=64)
+        v_scales = consts.tile([P, D], U8, align_bytes=64)
+        nc.vector.quantize_mx(
+            out=v_codes[:].bitcast(FP8X4),
+            scales=v_scales[:],
+            in_=v_t[:].rearrange("p c t -> p (c t)"),
+        )
+
+        acc_t = [acc_pool.tile([P, MOVING_TOKENS], F32, name="acc_t%d" % x) for x in range(D_HALVES)]
+        acc_last = acc_pool.tile([P, D], F32)
+
+        us_t = {}
+        us_codes = {}
+        us_scales = {}
+        h_t = {}
+        h_codes = {}
+        h_scales = {}
+        w_t = {}
+        w_codes = {}
+        w_scales = {}
+
+        def transpose_scale_u(g):
+            i, place = home[g]
+            u_words = u_rows[i][:].bitcast(F32)
+            us_t[g] = work.tile([P, K_PASS, PACK], BF16, name="us_t", align_bytes=64)
+            for k_half in range(2):
+                bank = ring.tile([P, 2, BANK_COLS], F32, tag="bank", name="u_bank")
+                for e in range(2):
+                    for half in range(2):
+                        first = (2 * k_half + e) * (RANK // 2)
+                        nc.tensor.transpose(
+                            bank[:, half, e * P : (e + 1) * P],
+                            u_words[:, place, first + half : first + RANK // 2 : 2],
+                            ident[:],
+                        )
+                cols = slice(k_half * BANK_COLS, (k_half + 1) * BANK_COLS)
+                nc.vector.tensor_tensor(
+                    out=us_t[g][:, cols, :].rearrange("p c (half e) -> p c half e", e=2),
+                    in0=bank[:].bitcast(BF16).rearrange("p half (c e) -> p c half e", e=2),
+                    in1=s_bank[:],
+                    op=mult,
+                )
+
+        def quantise_us(g):
+            us_codes[g] = work.tile([P, K_PASS], U32, name="us_codes", align_bytes=64)
+            us_scales[g] = work.tile([P, K_PASS], U8, name="us_scales", align_bytes=64)
+            nc.vector.quantize_mx(
+                out=us_codes[g][:].bitcast(FP8X4),
+                scales=us_scales[g][:],
+                in_=us_t[g][:].rearrange("p c t -> p (c t)"),
+            )
+
+        def transpose_h(g):
+            i, place = home[g]
+            h_words = h_rows[i][:].bitcast(F32)
+            h_t[g] = work.tile([P, TOKENS, PACK], BF16, name="h_t", align_bytes=64)
+            h_t_words = h_t[g][:].bitcast(F32)
+            for first_col in range(0, TOKENS, BANK_COLS):
+                cols = min(BANK_COLS, TOKENS - first_col)
+                bank = ring.tile([P, 2, BANK_COLS], F32, tag="bank", name="h_bank")
+                for y in range(cols // P):
+                    for half in range(2):
+                        first = place * (K_PASS // 2)
+                        nc.tensor.transpose(
+                            bank[:, half, y * P : (y + 1) * P],
+                            h_words[:, first_col // P + y, first + half : first + K_PASS // 2 : 2],
+                            ident[:],
+                        )
+                nc.scalar.copy(
+                    out=h_t_words[:, first_col : first_col + cols, :],
+                    in_=bank[:, :, 0:cols].rearrange("p half c -> p c half"),
+                )
+
+        def quantise_h(g):
+            h_codes[g] = work.tile([P, TOKENS], U32, name="h_codes", bufs=4, align_bytes=64)
+            h_scales[g] = work.tile([P, TOKENS], U8, name="h_scales", bufs=4, align_bytes=64)
+            for cols in (slice(0, MOVING_TOKENS), slice(MOVING_TOKENS, TOKENS)):
+                nc.vector.quantize_mx(
+                    out=h_codes[g][:, cols].bitcast(FP8X4),
+                    scales=h_scales[g][:, cols],
+                    in_=h_t[g][:, cols, :].rearrange("p c t -> p (c t)"),
+                )
+
+        def build_w(g):
+            w_t[g] = work.tile([P, D, PACK], BF16, name="w_t", align_bytes=64)
+            for x in range(D_HALVES):
+                d_cols = slice(x * P, (x + 1) * P)
+                bank = ring.tile([P, PACK, P], F32, tag="bank", name="w_bank")
+                for t in range(PACK):
+                    k_cols = slice(t * P, (t + 1) * P)
+                    nc.tensor.matmul_mx(
+                        out=bank[:, t, :],
+                        lhsT=us_codes[g][:, k_cols].bitcast(FP8X4),
+                        lhsT_scale=us_scales[g][:, k_cols],
+                        rhs=v_codes[:, d_cols].bitcast(FP8X4),
+                        rhs_scale=v_scales[:, d_cols],
+                        start=True,
+                        stop=True,
+                    )
+                nc.scalar.copy(out=w_t[g][:, d_cols, :], in_=bank[:].rearrange("p t d -> p d t"))
+
+        def quantise_w(g):
+            w_codes[g] = work.tile([P, D], U32, name="w_codes", align_bytes=64)
+            w_scales[g] = work.tile([P, D], U8, name="w_scales", align_bytes=64)
+            nc.vector.quantize_mx(
+                out=w_codes[g][:].bitcast(FP8X4),
+                scales=w_scales[g][:],
+                in_=w_t[g][:].rearrange("p d t -> p (d t)"),
+            )
+
+        def apply_w(g):
+            first_pass = g == 0
+            last_pass = g == PASSES - 1
+            moving = slice(0, MOVING_TOKENS)
+            last_block = slice(MOVING_TOKENS, TOKENS)
+            for x in range(D_HALVES):
+                d_cols = slice(x * P, (x + 1) * P)
+                nc.tensor.matmul_mx(
+                    out=acc_t[x][:],
+                    lhsT=w_codes[g][:, d_cols].bitcast(FP8X4),
+                    lhsT_scale=w_scales[g][:, d_cols],
+                    rhs=h_codes[g][:, moving].bitcast(FP8X4),
+                    rhs_scale=h_scales[g][:, moving],
+                    start=first_pass,
+                    stop=last_pass,
+                )
+            nc.tensor.matmul_mx(
+                out=acc_last[:],
+                lhsT=h_codes[g][:, last_block].bitcast(FP8X4),
+                lhsT_scale=h_scales[g][:, last_block],
+                rhs=w_codes[g][:].bitcast(FP8X4),
+                rhs_scale=w_scales[g][:],
+                start=first_pass,
+                stop=last_pass,
+            )
+
+        for turn in range(PASSES + 3):
+            if 3 <= turn:
+                quantise_w(turn - 3)
+            if 1 <= turn <= PASSES:
+                quantise_h(turn - 1)
+                quantise_us(turn - 1)
+            if turn < PASSES:
+                transpose_h(turn)
+                transpose_scale_u(turn)
+                i = home[turn][0]
+                if turn == load_end[i] - 1 and i + LOADS_AHEAD < len(load_first):
+                    load(i + LOADS_AHEAD)
+            if 2 <= turn <= PASSES + 1:
+                build_w(turn - 2)
+            if 3 <= turn:
+                apply_w(turn - 3)
+
+        result = consts.tile([P, TOKEN_BLOCKS, D], F32)
+        out_t = [consts.tile([P, MOVING_TOKENS], F32, name="out_t%d" % x) for x in range(D_HALVES)]
+        nc.scalar.copy(out=out_t[0][:], in_=acc_t[0][:])
+        nc.vector.tensor_copy(out=out_t[1][:], in_=acc_t[1][:])
+        nc.vector.tensor_tensor(
+            out=result[:, MOVING_BLOCKS, :], in0=acc_last[:], in1=bias_all[:], op=add
+        )
+        nc.sync.dma_start(out=out_view[:, MOVING_BLOCKS, :], in_=result[:, MOVING_BLOCKS, :])
+        blocks_per_bank = BANK_F32 // D
+        for first_block in range(0, MOVING_BLOCKS, blocks_per_bank):
+            bank = ring.tile([P, blocks_per_bank, D], F32, tag="bank", name="out_bank")
+            for y in range(blocks_per_bank):
+                tok_cols = slice((first_block + y) * P, (first_block + y + 1) * P)
+                for x in range(D_HALVES):
+                    nc.tensor.transpose(
+                        bank[:, y, x * P : (x + 1) * P], out_t[x][:, tok_cols], ident[:]
+                    )
+            blocks = slice(first_block, first_block + blocks_per_bank)
+            nc.vector.tensor_tensor(
+                out=result[:, blocks, :],
+                in0=bank[:],
+                in1=bias_all[:].unsqueeze(1).to_broadcast([P, blocks_per_bank, D]),
+                op=add,
+            )
+            nc.sync.dma_start(out=out_view[:, blocks, :], in_=result[:, blocks, :])

@@ -28,6 +28,8 @@ MOVING_BLOCKS = MOVING_TOKENS // P
 ACC_BANKS = D_HALVES + 1
 RING_BANKS = 8 - ACC_BANKS
 
+SORTED_BLOCKS = 2
+
 PASSES_PER_LOAD = 2
 LOADS_AHEAD = 6
 LOAD_K = PASSES_PER_LOAD * K_PASS
@@ -119,6 +121,8 @@ def tile_hybridsuperlayer_pb_k_kernel(
         acc_t = [acc_pool.tile([P, MOVING_TOKENS], F32, name="acc_t%d" % x) for x in range(D_HALVES)]
         acc_last = acc_pool.tile([P, D], F32)
 
+        u_sorted = {}
+        h_sorted = {}
         us_t = {}
         us_codes = {}
         us_scales = {}
@@ -129,18 +133,36 @@ def tile_hybridsuperlayer_pb_k_kernel(
         w_codes = {}
         w_scales = {}
 
-        def transpose_scale_u(g):
+        def reorder_u(g):
             i, place = home[g]
-            u_words = u_rows[i][:].bitcast(F32)
+            u_sorted[g] = work.tile([P, PACK, 2, P], F32, name="u_sorted")
+            nc.vector.tensor_copy(
+                out=u_sorted[g][:],
+                in_=u_rows[i][:, place, :].bitcast(F32).rearrange(
+                    "p (t w half) -> p t half w", t=PACK, half=2
+                ),
+            )
+
+        def reorder_h(g):
+            i, place = home[g]
+            h_sorted[g] = work.tile([P, SORTED_BLOCKS, 2, P], F32, name="h_sorted")
+            first = place * (K_PASS // 2)
+            nc.scalar.copy(
+                out=h_sorted[g][:],
+                in_=h_rows[i][:].bitcast(F32)[:, 0:SORTED_BLOCKS, first : first + K_PASS // 2].rearrange(
+                    "p b (w half) -> p b half w", half=2
+                ),
+            )
+
+        def transpose_scale_u(g):
             us_t[g] = work.tile([P, K_PASS, PACK], BF16, name="us_t", align_bytes=64)
             for k_half in range(2):
                 bank = ring.tile([P, 2, BANK_COLS], F32, tag="bank", name="u_bank")
                 for e in range(2):
                     for half in range(2):
-                        first = (2 * k_half + e) * (RANK // 2)
                         nc.tensor.transpose(
                             bank[:, half, e * P : (e + 1) * P],
-                            u_words[:, place, first + half : first + RANK // 2 : 2],
+                            u_sorted[g][:, 2 * k_half + e, half, :],
                             ident[:],
                         )
                 cols = slice(k_half * BANK_COLS, (k_half + 1) * BANK_COLS)
@@ -171,9 +193,14 @@ def tile_hybridsuperlayer_pb_k_kernel(
                 for y in range(cols // P):
                     for half in range(2):
                         first = place * (K_PASS // 2)
+                        b = first_col // P + y
+                        if b < SORTED_BLOCKS:
+                            words = h_sorted[g][:, b, half, :]
+                        else:
+                            words = h_words[:, b, first + half : first + K_PASS // 2 : 2]
                         nc.tensor.transpose(
                             bank[:, half, y * P : (y + 1) * P],
-                            h_words[:, first_col // P + y, first + half : first + K_PASS // 2 : 2],
+                            words,
                             ident[:],
                         )
                 nc.scalar.copy(
@@ -244,14 +271,21 @@ def tile_hybridsuperlayer_pb_k_kernel(
                 stop=last_pass,
             )
 
+        reorder_u(0)
+        reorder_h(0)
         for turn in range(PASSES + 3):
+            if 1 <= turn <= PASSES:
+                quantise_h(turn - 1)
             if 3 <= turn:
                 quantise_w(turn - 3)
             if 1 <= turn <= PASSES:
-                quantise_h(turn - 1)
                 quantise_us(turn - 1)
+            if turn + 1 < PASSES:
+                reorder_u(turn + 1)
             if turn < PASSES:
                 transpose_h(turn)
+                if turn + 1 < PASSES:
+                    reorder_h(turn + 1)
                 transpose_scale_u(turn)
                 i = home[turn][0]
                 if turn == load_end[i] - 1 and i + LOADS_AHEAD < len(load_first):

@@ -121,7 +121,6 @@ def tile_hybridsuperlayer_pb_k_kernel(
         acc_t = [acc_pool.tile([P, MOVING_TOKENS], F32, name="acc_t%d" % x) for x in range(D_HALVES)]
         acc_last = acc_pool.tile([P, D], F32)
 
-        u_sorted = {}
         h_sorted = {}
         us_t = {}
         us_codes = {}
@@ -132,16 +131,6 @@ def tile_hybridsuperlayer_pb_k_kernel(
         w_t = {}
         w_codes = {}
         w_scales = {}
-
-        def reorder_u(g):
-            i, place = home[g]
-            u_sorted[g] = work.tile([P, PACK, 2, P], F32, name="u_sorted")
-            nc.vector.tensor_copy(
-                out=u_sorted[g][:],
-                in_=u_rows[i][:, place, :].bitcast(F32).rearrange(
-                    "p (t w half) -> p t half w", t=PACK, half=2
-                ),
-            )
 
         def reorder_h(g):
             i, place = home[g]
@@ -155,14 +144,17 @@ def tile_hybridsuperlayer_pb_k_kernel(
             )
 
         def transpose_scale_u(g):
+            i, place = home[g]
+            u_words = u_rows[i][:].bitcast(F32)
             us_t[g] = work.tile([P, K_PASS, PACK], BF16, name="us_t", align_bytes=64)
             for k_half in range(2):
                 bank = ring.tile([P, 2, BANK_COLS], F32, tag="bank", name="u_bank")
                 for e in range(2):
                     for half in range(2):
+                        first = (2 * k_half + e) * (RANK // 2)
                         nc.tensor.transpose(
                             bank[:, half, e * P : (e + 1) * P],
-                            u_sorted[g][:, 2 * k_half + e, half, :],
+                            u_words[:, place, first + half : first + RANK // 2 : 2],
                             ident[:],
                         )
                 cols = slice(k_half * BANK_COLS, (k_half + 1) * BANK_COLS)
@@ -271,7 +263,6 @@ def tile_hybridsuperlayer_pb_k_kernel(
                 stop=last_pass,
             )
 
-        reorder_u(0)
         reorder_h(0)
         for turn in range(PASSES + 3):
             if 1 <= turn <= PASSES:
@@ -280,8 +271,6 @@ def tile_hybridsuperlayer_pb_k_kernel(
                 quantise_w(turn - 3)
             if 1 <= turn <= PASSES:
                 quantise_us(turn - 1)
-            if turn + 1 < PASSES:
-                reorder_u(turn + 1)
             if turn < PASSES:
                 transpose_h(turn)
                 if turn + 1 < PASSES:

@@ -28,7 +28,7 @@ MOVING_BLOCKS = MOVING_TOKENS // P
 ACC_BANKS = D_HALVES + 1
 RING_BANKS = 8 - ACC_BANKS
 
-SORTED_BLOCKS = 2
+SCALAR_BLOCKS = 3
 
 PASSES_PER_LOAD = 2
 LOADS_AHEAD = 6
@@ -121,7 +121,8 @@ def tile_hybridsuperlayer_pb_k_kernel(
         acc_t = [acc_pool.tile([P, MOVING_TOKENS], F32, name="acc_t%d" % x) for x in range(D_HALVES)]
         acc_last = acc_pool.tile([P, D], F32)
 
-        h_sorted = {}
+        h_sorted_first = {}
+        h_sorted_last = {}
         us_t = {}
         us_codes = {}
         us_scales = {}
@@ -132,36 +133,43 @@ def tile_hybridsuperlayer_pb_k_kernel(
         w_codes = {}
         w_scales = {}
 
-        def reorder_h(g):
+        def sort_h(g, engine_copy, tiles, blocks):
             i, place = home[g]
-            h_sorted[g] = work.tile([P, SORTED_BLOCKS, 2, P], F32, name="h_sorted")
+            width = blocks.stop - blocks.start
+            tiles[g] = work.tile([P, width, 2, P], F32, name="h_sorted_%d" % blocks.start)
             first = place * (K_PASS // 2)
-            nc.scalar.copy(
-                out=h_sorted[g][:],
-                in_=h_rows[i][:].bitcast(F32)[:, 0:SORTED_BLOCKS, first : first + K_PASS // 2].rearrange(
+            engine_copy(
+                out=tiles[g][:],
+                in_=h_rows[i][:].bitcast(F32)[:, blocks, first : first + K_PASS // 2].rearrange(
                     "p b (w half) -> p b half w", half=2
                 ),
             )
+
+        def sort_h_on_scalar(g):
+            sort_h(g, nc.scalar.copy, h_sorted_first, slice(0, SCALAR_BLOCKS))
+
+        def sort_h_on_vector(g):
+            sort_h(g, nc.vector.tensor_copy, h_sorted_last, slice(SCALAR_BLOCKS, TOKEN_BLOCKS))
 
         def transpose_scale_u(g):
             i, place = home[g]
             u_words = u_rows[i][:].bitcast(F32)
             us_t[g] = work.tile([P, K_PASS, PACK], BF16, name="us_t", align_bytes=64)
             for k_half in range(2):
-                bank = ring.tile([P, 2, BANK_COLS], F32, tag="bank", name="u_bank")
+                bank = ring.tile([P, BANK_COLS, 2], F32, tag="bank", name="u_bank")
                 for e in range(2):
                     for half in range(2):
                         first = (2 * k_half + e) * (RANK // 2)
                         nc.tensor.transpose(
-                            bank[:, half, e * P : (e + 1) * P],
+                            bank[:, e * P : (e + 1) * P, half],
                             u_words[:, place, first + half : first + RANK // 2 : 2],
                             ident[:],
                         )
                 cols = slice(k_half * BANK_COLS, (k_half + 1) * BANK_COLS)
                 nc.vector.tensor_tensor(
-                    out=us_t[g][:, cols, :].rearrange("p c (half e) -> p c half e", e=2),
-                    in0=bank[:].bitcast(BF16).rearrange("p half (c e) -> p c half e", e=2),
-                    in1=s_bank[:],
+                    out=us_t[g][:, cols, :].rearrange("p c t -> p (c t)"),
+                    in0=bank[:].rearrange("p c half -> p (c half)").bitcast(BF16),
+                    in1=s_bank[:].rearrange("p c half e -> p (c half e)"),
                     op=mult,
                 )
 
@@ -175,8 +183,6 @@ def tile_hybridsuperlayer_pb_k_kernel(
             )
 
         def transpose_h(g):
-            i, place = home[g]
-            h_words = h_rows[i][:].bitcast(F32)
             h_t[g] = work.tile([P, TOKENS, PACK], BF16, name="h_t", align_bytes=64)
             h_t_words = h_t[g][:].bitcast(F32)
             for first_col in range(0, TOKENS, BANK_COLS):
@@ -184,12 +190,11 @@ def tile_hybridsuperlayer_pb_k_kernel(
                 bank = ring.tile([P, 2, BANK_COLS], F32, tag="bank", name="h_bank")
                 for y in range(cols // P):
                     for half in range(2):
-                        first = place * (K_PASS // 2)
                         b = first_col // P + y
-                        if b < SORTED_BLOCKS:
-                            words = h_sorted[g][:, b, half, :]
+                        if b < SCALAR_BLOCKS:
+                            words = h_sorted_first[g][:, b, half, :]
                         else:
-                            words = h_words[:, b, first + half : first + K_PASS // 2 : 2]
+                            words = h_sorted_last[g][:, b - SCALAR_BLOCKS, half, :]
                         nc.tensor.transpose(
                             bank[:, half, y * P : (y + 1) * P],
                             words,
@@ -263,7 +268,8 @@ def tile_hybridsuperlayer_pb_k_kernel(
                 stop=last_pass,
             )
 
-        reorder_h(0)
+        sort_h_on_scalar(0)
+        sort_h_on_vector(0)
         for turn in range(PASSES + 3):
             if 1 <= turn <= PASSES:
                 quantise_h(turn - 1)
@@ -271,10 +277,12 @@ def tile_hybridsuperlayer_pb_k_kernel(
                 quantise_w(turn - 3)
             if 1 <= turn <= PASSES:
                 quantise_us(turn - 1)
+            if turn + 1 < PASSES:
+                sort_h_on_vector(turn + 1)
             if turn < PASSES:
                 transpose_h(turn)
                 if turn + 1 < PASSES:
-                    reorder_h(turn + 1)
+                    sort_h_on_scalar(turn + 1)
                 transpose_scale_u(turn)
                 i = home[turn][0]
                 if turn == load_end[i] - 1 and i + LOADS_AHEAD < len(load_first):

@@ -28,7 +28,9 @@ MOVING_BLOCKS = MOVING_TOKENS // P
 ACC_BANKS = D_HALVES + 1
 RING_BANKS = 8 - ACC_BANKS
 
-SCALAR_BLOCKS = 3
+SORT_AHEAD = 2
+FIRST_SORTED = 3
+SCALAR_BLOCKS = 2
 
 PASSES_PER_LOAD = 2
 LOADS_AHEAD = 6
@@ -69,27 +71,29 @@ def tile_hybridsuperlayer_pb_k_kernel(
             passes = load_end[i] - load_first[i]
             k_range = slice(load_first[i] * K_PASS, load_end[i] * K_PASS)
             h_rows[i] = loads.tile([P, TOKEN_BLOCKS, LOAD_K], BF16, name="h_rows")
-            nc.sync.dma_start(
-                out=h_rows[i][:, :, 0 : passes * K_PASS],
-                in_=h_flat[:, k_range].rearrange("(b p) k -> p b k", p=P),
-            )
+            first_blocks = range(0, TOKEN_BLOCKS, BANK_COLS // P if i == 0 else TOKEN_BLOCKS)
+            for first, end in zip(first_blocks, list(first_blocks)[1:] + [TOKEN_BLOCKS]):
+                nc.sync.dma_start(
+                    out=h_rows[i][:, first:end, 0 : passes * K_PASS],
+                    in_=h_flat[first * P : end * P, k_range].rearrange("(b p) k -> p b k", p=P),
+                )
             u_rows[i] = loads.tile([P, PASSES_PER_LOAD, PACK * RANK], BF16, name="u_rows")
             nc.sync.dma_start(
                 out=u_rows[i][:, 0:passes, :],
                 in_=c_proj_U[k_range, :].rearrange("(x p t) r -> p x (t r)", p=P, t=PACK),
             )
 
-        v_rows = consts.tile([P, D_HALVES, RANK], BF16)
-        nc.scalar.dma_start(out=v_rows[:], in_=c_proj_V.rearrange("(x p) r -> p x r", p=P))
         s_word = consts.tile([P, 2, 2], BF16)
         with nc.allow_non_contiguous_dma(reason="512 values, two pairs to a partition, once"):
             nc.scalar.dma_start(
                 out=s_word[:], in_=c_proj_S.rearrange("(p half e) -> p half e", half=2, p=P, e=2)
             )
-        bias_all = consts.tile([P, D], BF16)
-        nc.scalar.dma_start(out=bias_all[:], in_=c_proj_bias.partition_broadcast(P))
-        for i in range(LOADS_AHEAD):
+        load(0)
+        v_rows = consts.tile([P, D_HALVES, RANK], BF16)
+        nc.sync.dma_start(out=v_rows[:], in_=c_proj_V.rearrange("(x p) r -> p x r", p=P))
+        for i in range(1, LOADS_AHEAD):
             load(i)
+        bias_all = consts.tile([P, D], BF16)
 
         ident = consts.tile([P, P], F32)
         make_identity(nc, ident[:])
@@ -99,24 +103,28 @@ def tile_hybridsuperlayer_pb_k_kernel(
             out=s_bank[:], in_=s_word[:].unsqueeze(1).to_broadcast([P, BANK_COLS, 2, 2])
         )
 
-        v_words = v_rows[:].bitcast(F32)
-        v_bank = ring.tile([P, 2, BANK_COLS], F32, tag="bank")
-        for x in range(D_HALVES):
-            for half in range(2):
-                nc.tensor.transpose(
-                    v_bank[:, half, x * P : (x + 1) * P],
-                    v_words[:, x, half : RANK // 2 : 2],
-                    ident[:],
-                )
         v_t = consts.tile([P, D, PACK], BF16, align_bytes=64)
-        nc.scalar.copy(out=v_t[:].bitcast(F32), in_=v_bank[:].rearrange("p half c -> p c half"))
         v_codes = consts.tile([P, D], U32, align_bytes=64)
         v_scales = consts.tile([P, D], U8, align_bytes=64)
-        nc.vector.quantize_mx(
-            out=v_codes[:].bitcast(FP8X4),
-            scales=v_scales[:],
-            in_=v_t[:].rearrange("p c t -> p (c t)"),
-        )
+
+        def transpose_v():
+            v_words = v_rows[:].bitcast(F32)
+            bank = ring.tile([P, 2, BANK_COLS], F32, tag="bank", name="v_bank")
+            for x in range(D_HALVES):
+                for half in range(2):
+                    nc.tensor.transpose(
+                        bank[:, half, x * P : (x + 1) * P],
+                        v_words[:, x, half : RANK // 2 : 2],
+                        ident[:],
+                    )
+            nc.scalar.copy(out=v_t[:].bitcast(F32), in_=bank[:].rearrange("p half c -> p c half"))
+
+        def quantise_v():
+            nc.vector.quantize_mx(
+                out=v_codes[:].bitcast(FP8X4),
+                scales=v_scales[:],
+                in_=v_t[:].rearrange("p c t -> p (c t)"),
+            )
 
         acc_t = [acc_pool.tile([P, MOVING_TOKENS], F32, name="acc_t%d" % x) for x in range(D_HALVES)]
         acc_last = acc_pool.tile([P, D], F32)
@@ -139,9 +147,9 @@ def tile_hybridsuperlayer_pb_k_kernel(
             tiles[g] = work.tile([P, width, 2, P], F32, name="h_sorted_%d" % blocks.start)
             first = place * (K_PASS // 2)
             engine_copy(
-                out=tiles[g][:],
+                out=tiles[g][:].rearrange("p b half w -> p half b w"),
                 in_=h_rows[i][:].bitcast(F32)[:, blocks, first : first + K_PASS // 2].rearrange(
-                    "p b (w half) -> p b half w", half=2
+                    "p b (w half) -> p half b w", half=2
                 ),
             )
 
@@ -183,6 +191,8 @@ def tile_hybridsuperlayer_pb_k_kernel(
             )
 
         def transpose_h(g):
+            i, place = home[g]
+            h_words = h_rows[i][:].bitcast(F32)
             h_t[g] = work.tile([P, TOKENS, PACK], BF16, name="h_t", align_bytes=64)
             h_t_words = h_t[g][:].bitcast(F32)
             for first_col in range(0, TOKENS, BANK_COLS):
@@ -191,7 +201,10 @@ def tile_hybridsuperlayer_pb_k_kernel(
                 for y in range(cols // P):
                     for half in range(2):
                         b = first_col // P + y
-                        if b < SCALAR_BLOCKS:
+                        if g < FIRST_SORTED:
+                            first = place * (K_PASS // 2)
+                            words = h_words[:, b, first + half : first + K_PASS // 2 : 2]
+                        elif b < SCALAR_BLOCKS:
                             words = h_sorted_first[g][:, b, half, :]
                         else:
                             words = h_sorted_last[g][:, b - SCALAR_BLOCKS, half, :]
@@ -215,7 +228,7 @@ def tile_hybridsuperlayer_pb_k_kernel(
                     in_=h_t[g][:, cols, :].rearrange("p c t -> p (c t)"),
                 )
 
-        def build_w(g):
+        def build_w(g, second_copy):
             w_t[g] = work.tile([P, D, PACK], BF16, name="w_t", align_bytes=64)
             for x in range(D_HALVES):
                 d_cols = slice(x * P, (x + 1) * P)
@@ -231,7 +244,8 @@ def tile_hybridsuperlayer_pb_k_kernel(
                         start=True,
                         stop=True,
                     )
-                nc.scalar.copy(out=w_t[g][:, d_cols, :], in_=bank[:].rearrange("p t d -> p d t"))
+                engine_copy = nc.scalar.copy if x == 0 else second_copy
+                engine_copy(out=w_t[g][:, d_cols, :], in_=bank[:].rearrange("p t d -> p d t"))
 
         def quantise_w(g):
             w_codes[g] = work.tile([P, D], U32, name="w_codes", align_bytes=64)
@@ -268,29 +282,41 @@ def tile_hybridsuperlayer_pb_k_kernel(
                 stop=last_pass,
             )
 
-        sort_h_on_scalar(0)
-        sort_h_on_vector(0)
-        for turn in range(PASSES + 3):
-            if 1 <= turn <= PASSES:
+        for turn in range(PASSES):
+            if 1 <= turn:
                 quantise_h(turn - 1)
             if 3 <= turn:
                 quantise_w(turn - 3)
-            if 1 <= turn <= PASSES:
+            if 1 <= turn:
                 quantise_us(turn - 1)
-            if turn + 1 < PASSES:
-                sort_h_on_vector(turn + 1)
-            if turn < PASSES:
-                transpose_h(turn)
-                if turn + 1 < PASSES:
-                    sort_h_on_scalar(turn + 1)
-                transpose_scale_u(turn)
-                i = home[turn][0]
-                if turn == load_end[i] - 1 and i + LOADS_AHEAD < len(load_first):
-                    load(i + LOADS_AHEAD)
-            if 2 <= turn <= PASSES + 1:
-                build_w(turn - 2)
+            transpose_h(turn)
+            if FIRST_SORTED <= turn + SORT_AHEAD < PASSES:
+                sort_h_on_scalar(turn + SORT_AHEAD)
+            transpose_scale_u(turn)
+            if FIRST_SORTED <= turn + SORT_AHEAD < PASSES:
+                sort_h_on_vector(turn + SORT_AHEAD)
+            if turn == 0:
+                transpose_v()
+                quantise_v()
+            i = home[turn][0]
+            if turn == load_end[i] - 1 and i + LOADS_AHEAD < len(load_first):
+                load(i + LOADS_AHEAD)
+            if turn == LOADS_AHEAD:
+                nc.sync.dma_start(out=bias_all[:], in_=c_proj_bias.partition_broadcast(P))
+            if 2 <= turn:
+                build_w(turn - 2, nc.scalar.copy)
             if 3 <= turn:
                 apply_w(turn - 3)
+
+        quantise_us(PASSES - 1)
+        quantise_w(PASSES - 3)
+        build_w(PASSES - 2, nc.vector.tensor_copy)
+        build_w(PASSES - 1, nc.vector.tensor_copy)
+        quantise_h(PASSES - 1)
+        quantise_w(PASSES - 2)
+        quantise_w(PASSES - 1)
+        for g in range(PASSES - 3, PASSES):
+            apply_w(g)
 
         result = consts.tile([P, TOKEN_BLOCKS, D], F32)
         out_t = [consts.tile([P, MOVING_TOKENS], F32, name="out_t%d" % x) for x in range(D_HALVES)]

@@ -31,6 +31,7 @@ RING_BANKS = 8 - ACC_BANKS
 SORT_AHEAD = 2
 FIRST_SORTED = 3
 SCALAR_BLOCKS = 2
+SORTED_BLOCKS = 3
 
 PASSES_PER_LOAD = 2
 LOADS_AHEAD = 6
@@ -157,27 +158,27 @@ def tile_hybridsuperlayer_pb_k_kernel(
             sort_h(g, nc.scalar.copy, h_sorted_first, slice(0, SCALAR_BLOCKS))
 
         def sort_h_on_vector(g):
-            sort_h(g, nc.vector.tensor_copy, h_sorted_last, slice(SCALAR_BLOCKS, TOKEN_BLOCKS))
+            sort_h(g, nc.vector.tensor_copy, h_sorted_last, slice(SCALAR_BLOCKS, SORTED_BLOCKS))
 
         def transpose_scale_u(g):
             i, place = home[g]
             u_words = u_rows[i][:].bitcast(F32)
             us_t[g] = work.tile([P, K_PASS, PACK], BF16, name="us_t", align_bytes=64)
             for k_half in range(2):
-                bank = ring.tile([P, BANK_COLS, 2], F32, tag="bank", name="u_bank")
+                bank = ring.tile([P, 2, BANK_COLS], F32, tag="bank", name="u_bank")
                 for e in range(2):
                     for half in range(2):
                         first = (2 * k_half + e) * (RANK // 2)
                         nc.tensor.transpose(
-                            bank[:, e * P : (e + 1) * P, half],
+                            bank[:, half, e * P : (e + 1) * P],
                             u_words[:, place, first + half : first + RANK // 2 : 2],
                             ident[:],
                         )
                 cols = slice(k_half * BANK_COLS, (k_half + 1) * BANK_COLS)
                 nc.vector.tensor_tensor(
-                    out=us_t[g][:, cols, :].rearrange("p c t -> p (c t)"),
-                    in0=bank[:].rearrange("p c half -> p (c half)").bitcast(BF16),
-                    in1=s_bank[:].rearrange("p c half e -> p (c half e)"),
+                    out=us_t[g][:, cols, :].rearrange("p c (half e) -> p c half e", e=2),
+                    in0=bank[:].bitcast(BF16).rearrange("p half (c e) -> p c half e", e=2),
+                    in1=s_bank[:],
                     op=mult,
                 )
 
@@ -201,7 +202,7 @@ def tile_hybridsuperlayer_pb_k_kernel(
                 for y in range(cols // P):
                     for half in range(2):
                         b = first_col // P + y
-                        if g < FIRST_SORTED:
+                        if g < FIRST_SORTED or b >= SORTED_BLOCKS:
                             first = place * (K_PASS // 2)
                             words = h_words[:, b, first + half : first + K_PASS // 2 : 2]
                         elif b < SCALAR_BLOCKS:

from contextlib import ExitStack

import concourse.mybir as mybir
from concourse.masks import make_identity

BF16 = mybir.dt.bfloat16
F32 = mybir.dt.float32
U32 = mybir.dt.uint32
U8 = mybir.dt.uint8
FP8X4 = mybir.dt.float8_e4m3fn_x4

P = 128
PACK = 4
K_PASS = P * PACK

TOKENS = 640
TOKEN_BLOCKS = TOKENS // P
DFF = 16384
RANK = 512
D = 256
D_HALVES = D // P
PASSES = DFF // K_PASS

BANK_F32 = 512
BANK_COLS = BANK_F32 // 2
MOVING_TOKENS = BANK_F32
MOVING_BLOCKS = MOVING_TOKENS // P
ACC_BANKS = D_HALVES + 1
RING_BANKS = 8 - ACC_BANKS

SORT_AHEAD = 2
FIRST_SORTED = 3
SCALAR_BLOCKS = 2
SORTED_BLOCKS = 3

PASSES_PER_LOAD = 2
LOADS_AHEAD = 6
LOAD_K = PASSES_PER_LOAD * K_PASS

FLOPS = 2 * DFF * RANK * D + 2 * TOKENS * DFF * D


def tile_hybridsuperlayer_pb_k_kernel(
    tc, h_gelu, c_proj_U, c_proj_S, c_proj_V, c_proj_bias, out
):
    nc = tc.nc
    mult = mybir.AluOpType.mult
    add = mybir.AluOpType.add

    h_flat = h_gelu.flatten_outer_dims()
    out_view = out.flatten_outer_dims().rearrange("(b p) d -> p b d", p=P)

    load_first = list(range(PASSES_PER_LOAD)) + list(range(PASSES_PER_LOAD, PASSES, PASSES_PER_LOAD))
    load_end = load_first[1:] + [PASSES]
    home = {}
    for i in range(len(load_first)):
        for g in range(load_first[i], load_end[i]):
            home[g] = (i, g - load_first[i])

    with ExitStack() as ctx:
        consts = ctx.enter_context(tc.tile_pool(name="consts", bufs=1))
        loads = ctx.enter_context(tc.tile_pool(name="loads", bufs=LOADS_AHEAD))
        work = ctx.enter_context(tc.tile_pool(name="work", bufs=3))
        acc_pool = ctx.enter_context(tc.psum_pool(name="acc", bufs=1))
        ring = ctx.enter_context(tc.psum_pool(name="ring", bufs=RING_BANKS))
        ctx.enter_context(tc.manual_schedule())

        u_rows = {}
        h_rows = {}

        def load(i):
            passes = load_end[i] - load_first[i]
            k_range = slice(load_first[i] * K_PASS, load_end[i] * K_PASS)
            h_rows[i] = loads.tile([P, TOKEN_BLOCKS, LOAD_K], BF16, name="h_rows")
            first_blocks = range(0, TOKEN_BLOCKS, BANK_COLS // P if i == 0 else TOKEN_BLOCKS)
            for first, end in zip(first_blocks, list(first_blocks)[1:] + [TOKEN_BLOCKS]):
                nc.sync.dma_start(
                    out=h_rows[i][:, first:end, 0 : passes * K_PASS],
                    in_=h_flat[first * P : end * P, k_range].rearrange("(b p) k -> p b k", p=P),
                )
            u_rows[i] = loads.tile([P, PASSES_PER_LOAD, PACK * RANK], BF16, name="u_rows")
            nc.sync.dma_start(
                out=u_rows[i][:, 0:passes, :],
                in_=c_proj_U[k_range, :].rearrange("(x p t) r -> p x (t r)", p=P, t=PACK),
            )

        s_word = consts.tile([P, 2, 2], BF16)
        with nc.allow_non_contiguous_dma(reason="512 values, two pairs to a partition, once"):
            nc.scalar.dma_start(
                out=s_word[:], in_=c_proj_S.rearrange("(p half e) -> p half e", half=2, p=P, e=2)
            )
        load(0)
        v_rows = consts.tile([P, D_HALVES, RANK], BF16)
        nc.sync.dma_start(out=v_rows[:], in_=c_proj_V.rearrange("(x p) r -> p x r", p=P))
        for i in range(1, LOADS_AHEAD):
            load(i)
        bias_all = consts.tile([P, D], BF16)

        ident = consts.tile([P, P], F32)
        make_identity(nc, ident[:])

        s_bank = consts.tile([P, BANK_COLS, 2, 2], BF16)
        nc.vector.tensor_copy(
            out=s_bank[:], in_=s_word[:].unsqueeze(1).to_broadcast([P, BANK_COLS, 2, 2])
        )

        v_t = consts.tile([P, D, PACK], BF16, align_bytes=64)
        v_codes = consts.tile([P, D], U32, align_bytes=64)
        v_scales = consts.tile([P, D], U8, align_bytes=64)

        def transpose_v():
            v_words = v_rows[:].bitcast(F32)
            bank = ring.tile([P, 2, BANK_COLS], F32, tag="bank", name="v_bank")
            for x in range(D_HALVES):
                for half in range(2):
                    nc.tensor.transpose(
                        bank[:, half, x * P : (x + 1) * P],
                        v_words[:, x, half : RANK // 2 : 2],
                        ident[:],
                    )
            nc.scalar.copy(out=v_t[:].bitcast(F32), in_=bank[:].rearrange("p half c -> p c half"))

        def quantise_v():
            nc.vector.quantize_mx(
                out=v_codes[:].bitcast(FP8X4),
                scales=v_scales[:],
                in_=v_t[:].rearrange("p c t -> p (c t)"),
            )

        acc_t = [acc_pool.tile([P, MOVING_TOKENS], F32, name="acc_t%d" % x) for x in range(D_HALVES)]
        acc_last = acc_pool.tile([P, D], F32)

        h_sorted_first = {}
        h_sorted_last = {}
        us_t = {}
        us_codes = {}
        us_scales = {}
        h_t = {}
        h_codes = {}
        h_scales = {}
        w_t = {}
        w_codes = {}
        w_scales = {}

        def sort_h(g, engine_copy, tiles, blocks):
            i, place = home[g]
            width = blocks.stop - blocks.start
            tiles[g] = work.tile([P, width, 2, P], F32, name="h_sorted_%d" % blocks.start)
            first = place * (K_PASS // 2)
            engine_copy(
                out=tiles[g][:].rearrange("p b half w -> p half b w"),
                in_=h_rows[i][:].bitcast(F32)[:, blocks, first : first + K_PASS // 2].rearrange(
                    "p b (w half) -> p half b w", half=2
                ),
            )

        def sort_h_on_scalar(g):
            sort_h(g, nc.scalar.copy, h_sorted_first, slice(0, SCALAR_BLOCKS))

        def sort_h_on_vector(g):
            sort_h(g, nc.vector.tensor_copy, h_sorted_last, slice(SCALAR_BLOCKS, SORTED_BLOCKS))

        def transpose_scale_u(g):
            i, place = home[g]
            u_words = u_rows[i][:].bitcast(F32)
            us_t[g] = work.tile([P, K_PASS, PACK], BF16, name="us_t", align_bytes=64)
            for k_half in range(2):
                bank = ring.tile([P, 2, BANK_COLS], F32, tag="bank", name="u_bank")
                for e in range(2):
                    for half in range(2):
                        first = (2 * k_half + e) * (RANK // 2)
                        nc.tensor.transpose(
                            bank[:, half, e * P : (e + 1) * P],
                            u_words[:, place, first + half : first + RANK // 2 : 2],
                            ident[:],
                        )
                cols = slice(k_half * BANK_COLS, (k_half + 1) * BANK_COLS)
                nc.vector.tensor_tensor(
                    out=us_t[g][:, cols, :].rearrange("p c (half e) -> p c half e", e=2),
                    in0=bank[:].bitcast(BF16).rearrange("p half (c e) -> p c half e", e=2),
                    in1=s_bank[:],
                    op=mult,
                )

        def quantise_us(g):
            us_codes[g] = work.tile([P, K_PASS], U32, name="us_codes", align_bytes=64)
            us_scales[g] = work.tile([P, K_PASS], U8, name="us_scales", align_bytes=64)
            nc.vector.quantize_mx(
                out=us_codes[g][:].bitcast(FP8X4),
                scales=us_scales[g][:],
                in_=us_t[g][:].rearrange("p c t -> p (c t)"),
            )

        def transpose_h(g):
            i, place = home[g]
            h_words = h_rows[i][:].bitcast(F32)
            h_t[g] = work.tile([P, TOKENS, PACK], BF16, name="h_t", align_bytes=64)
            h_t_words = h_t[g][:].bitcast(F32)
            for first_col in range(0, TOKENS, BANK_COLS):
                cols = min(BANK_COLS, TOKENS - first_col)
                bank = ring.tile([P, 2, BANK_COLS], F32, tag="bank", name="h_bank")
                for y in range(cols // P):
                    for half in range(2):
                        b = first_col // P + y
                        if g < FIRST_SORTED or b >= SORTED_BLOCKS:
                            first = place * (K_PASS // 2)
                            words = h_words[:, b, first + half : first + K_PASS // 2 : 2]
                        elif b < SCALAR_BLOCKS:
                            words = h_sorted_first[g][:, b, half, :]
                        else:
                            words = h_sorted_last[g][:, b - SCALAR_BLOCKS, half, :]
                        nc.tensor.transpose(
                            bank[:, half, y * P : (y + 1) * P],
                            words,
                            ident[:],
                        )
                nc.scalar.copy(
                    out=h_t_words[:, first_col : first_col + cols, :],
                    in_=bank[:, :, 0:cols].rearrange("p half c -> p c half"),
                )

        def quantise_h(g):
            h_codes[g] = work.tile([P, TOKENS], U32, name="h_codes", bufs=4, align_bytes=64)
            h_scales[g] = work.tile([P, TOKENS], U8, name="h_scales", bufs=4, align_bytes=64)
            for cols in (slice(0, MOVING_TOKENS), slice(MOVING_TOKENS, TOKENS)):
                nc.vector.quantize_mx(
                    out=h_codes[g][:, cols].bitcast(FP8X4),
                    scales=h_scales[g][:, cols],
                    in_=h_t[g][:, cols, :].rearrange("p c t -> p (c t)"),
                )

        def build_w(g, second_copy):
            w_t[g] = work.tile([P, D, PACK], BF16, name="w_t", align_bytes=64)
            for x in range(D_HALVES):
                d_cols = slice(x * P, (x + 1) * P)
                bank = ring.tile([P, PACK, P], F32, tag="bank", name="w_bank")
                for t in range(PACK):
                    k_cols = slice(t * P, (t + 1) * P)
                    nc.tensor.matmul_mx(
                        out=bank[:, t, :],
                        lhsT=us_codes[g][:, k_cols].bitcast(FP8X4),
                        lhsT_scale=us_scales[g][:, k_cols],
                        rhs=v_codes[:, d_cols].bitcast(FP8X4),
                        rhs_scale=v_scales[:, d_cols],
                        start=True,
                        stop=True,
                    )
                engine_copy = nc.scalar.copy if x == 0 else second_copy
                engine_copy(out=w_t[g][:, d_cols, :], in_=bank[:].rearrange("p t d -> p d t"))

        def quantise_w(g):
            w_codes[g] = work.tile([P, D], U32, name="w_codes", align_bytes=64)
            w_scales[g] = work.tile([P, D], U8, name="w_scales", align_bytes=64)
            nc.vector.quantize_mx(
                out=w_codes[g][:].bitcast(FP8X4),
                scales=w_scales[g][:],
                in_=w_t[g][:].rearrange("p d t -> p (d t)"),
            )

        def apply_w(g):
            first_pass = g == 0
            last_pass = g == PASSES - 1
            moving = slice(0, MOVING_TOKENS)
            last_block = slice(MOVING_TOKENS, TOKENS)
            for x in range(D_HALVES):
                d_cols = slice(x * P, (x + 1) * P)
                nc.tensor.matmul_mx(
                    out=acc_t[x][:],
                    lhsT=w_codes[g][:, d_cols].bitcast(FP8X4),
                    lhsT_scale=w_scales[g][:, d_cols],
                    rhs=h_codes[g][:, moving].bitcast(FP8X4),
                    rhs_scale=h_scales[g][:, moving],
                    start=first_pass,
                    stop=last_pass,
                )
            nc.tensor.matmul_mx(
                out=acc_last[:],
                lhsT=h_codes[g][:, last_block].bitcast(FP8X4),
                lhsT_scale=h_scales[g][:, last_block],
                rhs=w_codes[g][:].bitcast(FP8X4),
                rhs_scale=w_scales[g][:],
                start=first_pass,
                stop=last_pass,
            )

        for turn in range(PASSES):
            if 1 <= turn:
                quantise_h(turn - 1)
            if 3 <= turn:
                quantise_w(turn - 3)
            if 1 <= turn:
                quantise_us(turn - 1)
            transpose_h(turn)
            if FIRST_SORTED <= turn + SORT_AHEAD < PASSES:
                sort_h_on_scalar(turn + SORT_AHEAD)
            transpose_scale_u(turn)
            if FIRST_SORTED <= turn + SORT_AHEAD < PASSES:
                sort_h_on_vector(turn + SORT_AHEAD)
            if turn == 0:
                transpose_v()
                quantise_v()
            i = home[turn][0]
            if turn == load_end[i] - 1 and i + LOADS_AHEAD < len(load_first):
                load(i + LOADS_AHEAD)
            if turn == LOADS_AHEAD:
                nc.sync.dma_start(out=bias_all[:], in_=c_proj_bias.partition_broadcast(P))
            if 2 <= turn:
                build_w(turn - 2, nc.scalar.copy)
            if 3 <= turn:
                apply_w(turn - 3)

        quantise_us(PASSES - 1)
        quantise_w(PASSES - 3)
        build_w(PASSES - 2, nc.vector.tensor_copy)
        build_w(PASSES - 1, nc.vector.tensor_copy)
        quantise_h(PASSES - 1)
        quantise_w(PASSES - 2)
        quantise_w(PASSES - 1)
        for g in range(PASSES - 3, PASSES):
            apply_w(g)

        result = consts.tile([P, TOKEN_BLOCKS, D], F32)
        out_t = [consts.tile([P, MOVING_TOKENS], F32, name="out_t%d" % x) for x in range(D_HALVES)]
        nc.scalar.copy(out=out_t[0][:], in_=acc_t[0][:])
        nc.vector.tensor_copy(out=out_t[1][:], in_=acc_t[1][:])
        nc.vector.tensor_tensor(
            out=result[:, MOVING_BLOCKS, :], in0=acc_last[:], in1=bias_all[:], op=add
        )
        nc.sync.dma_start(out=out_view[:, MOVING_BLOCKS, :], in_=result[:, MOVING_BLOCKS, :])
        blocks_per_bank = BANK_F32 // D
        for first_block in range(0, MOVING_BLOCKS, blocks_per_bank):
            bank = ring.tile([P, blocks_per_bank, D], F32, tag="bank", name="out_bank")
            for y in range(blocks_per_bank):
                tok_cols = slice((first_block + y) * P, (first_block + y + 1) * P)
                for x in range(D_HALVES):
                    nc.tensor.transpose(
                        bank[:, y, x * P : (x + 1) * P], out_t[x][:, tok_cols], ident[:]
                    )
            blocks = slice(first_block, first_block + blocks_per_bank)
            nc.vector.tensor_tensor(
                out=result[:, blocks, :],
                in0=bank[:],
                in1=bias_all[:].unsqueeze(1).to_broadcast([P, blocks_per_bank, D]),
                op=add,
            )
            nc.sync.dma_start(out=out_view[:, blocks, :], in_=result[:, blocks, :])
